import numpy as np
import ml_dtypes


def mxq(x, axis, fmt="e4m3"):
    dtype, down = {"e4m3": (ml_dtypes.float8_e4m3fn, 7), "e5m2": (ml_dtypes.float8_e5m2, 14)}[fmt]
    v = np.moveaxis(np.asarray(x, np.float32).astype(ml_dtypes.bfloat16).astype(np.float64), axis, -1)
    blocks = v.reshape(v.shape[:-1] + (-1, 32))
    amax = np.abs(blocks).max(-1, keepdims=True)
    byte = np.maximum(np.where(amax > 0, np.frexp(amax)[1] - 1 + 127, 0) - down, 1)
    scale = np.exp2(byte - 127.0)
    codes = (blocks / scale).astype(np.float32).astype(dtype).astype(np.float64)
    return np.moveaxis((codes * scale).reshape(v.shape), -1, axis)


WIDE = False


def mx_kscale(k):
    if not WIDE:
        return np.ones(k)
    levels = np.array([10, -10, 5, -5, 0])
    a = np.random.permutation(np.resize(levels, k // 512 * 4)).reshape(k // 512, 4)
    idx = np.arange(k)
    return np.exp2(a[idx // 512, idx % 128 // 32])


BF16 = ml_dtypes.bfloat16


def bf(x):
    return np.asarray(x, np.float32).astype(BF16)


def f64(x):
    return np.asarray(x).astype(np.float64)


B, S, D, F, F2 = 4, 256, 512, 2048, 1024
EPS = 1e-6
D2 = 2 * D


def setup_inputs():
    n = np.random.standard_normal
    s, t = mx_kscale(F), mx_kscale(D2)
    tr, ti = t[:D], t[D:]
    wd = 1.5 / np.sqrt(F)
    return {'h_r': bf(n((B, S, F)) * 0.6 * s), 'h_i': bf(n((B, S, F)) * 0.6 * s),
            'w2r': bf(n((F, D)) * wd / s[:, None] * tr), 'b2r': bf(n(D) * 0.2 * tr),
            'w2i': bf(n((F, D)) * wd / s[:, None] * ti), 'b2i': bf(n(D) * 0.2 * ti),
            'We': bf(n((D2, D)) / np.sqrt(D2) / t[:, None]), 'be': bf(n(D) * 0.2),
            'g_rms': bf(1.0 + 0.1 * n(D))}


def reference(h_r, h_i, w2r, b2r, w2i, b2i, We, be, g_rms):
    rp = (mxq(f64(h_r), 2, 'e4m3') @ mxq(f64(w2r), 0, 'e4m3')) + f64(b2r)
    ip = (mxq(f64(h_i), 2, 'e4m3') @ mxq(f64(w2i), 0, 'e4m3')) + f64(b2i)
    cat = np.concatenate([rp, ip], axis=-1)
    wave = (mxq(cat, 2, 'e4m3') @ mxq(f64(We), 0, 'e4m3')) + f64(be)
    return wave * (1.0 / np.sqrt(np.mean(wave * wave, axis=-1, keepdims=True) + EPS)) * f64(g_rms)

@@ -1,0 +1,273 @@
+from contextlib import ExitStack
+
+import concourse.mybir as mybir
+from concourse.masks import make_identity
+
+F32 = mybir.dt.float32
+BF16 = mybir.dt.bfloat16
+U32 = mybir.dt.uint32
+U8 = mybir.dt.uint8
+FP8X4 = mybir.dt.float8_e4m3fn_x4
+ACT = mybir.ActivationFunctionType
+ALU = mybir.AluOpType
+
+P = 128
+PACK = 4
+K_PASS = P * PACK
+TOKENS = 1024
+F = 2048
+D = 512
+EPS = 1e-6
+
+STREAMS = 2
+PASSES = F // K_PASS
+D_TILES = D // P
+TOKEN_TILES = TOKENS // P
+TILES = 2
+QUARTERS = TOKEN_TILES // TILES
+COLS = TILES * P
+VECTOR_COLS = 384
+
+FLOPS = 2 * TOKENS * F * D * STREAMS + 2 * TOKENS * (STREAMS * D) * D
+
+
+def regroup(copy, grouped, rows, first_col, last_col):
+    src = rows.rearrange("p (t c i) -> p c t i", t=PACK, i=4)
+    dst = grouped.rearrange("p (c i t) -> p c t i", i=4, t=PACK)
+    copy(out=dst[:, first_col // 4 : last_col // 4], in_=src[:, first_col // 4 : last_col // 4])
+
+
+def tile_wavenetworklm_pb_kernel(tc, h_r, h_i, w2r, b2r, w2i, b2i, We, be, g_rms, out):
+    nc = tc.nc
+    hidden = (h_r, h_i)
+    weights = (w2r, w2i)
+    biases = (b2r, b2i)
+
+    with ExitStack() as ctx:
+        const = ctx.enter_context(tc.tile_pool(name="const", bufs=1))
+        raw = ctx.enter_context(tc.tile_pool(name="raw", bufs=1))
+        keep = ctx.enter_context(tc.tile_pool(name="keep", bufs=1))
+        stage = ctx.enter_context(tc.tile_pool(name="stage", bufs=3))
+        tail = ctx.enter_context(tc.tile_pool(name="tail", bufs=2))
+        acc_pool = ctx.enter_context(tc.psum_pool(name="acc", bufs=1))
+        work_pool = ctx.enter_context(tc.psum_pool(name="work", bufs=4))
+
+        h_raw = {}
+        w_raw = {}
+
+        def load_hidden(s, q):
+            view = hidden[s].flatten_outer_dims().rearrange("(p j) k -> p (j k)", j=TOKEN_TILES)
+            t = raw.tile([P, TILES * F], BF16, name="h_raw_%d_%d" % (s, q))
+            nc.sync.dma_start(out=t[:], in_=view[:, TILES * F * q : TILES * F * (q + 1)])
+            h_raw[(s, q)] = t
+
+        def load_weights(s, g):
+            view = weights[s].rearrange("(c q e) n -> q c (e n)", q=P, e=2)
+            t = raw.tile([P, PACK * D], BF16, name="w_raw_%d_%d" % (s, g))
+            nc.sync.dma_start(
+                out=t[:].rearrange("p (u x) -> p u x", u=2), in_=view[:, 2 * g : 2 * g + 2, :]
+            )
+            w_raw[(s, g)] = t
+
+        load_hidden(0, 0)
+        for g in range(PASSES):
+            load_weights(0, g)
+        load_hidden(0, 1)
+        load_weights(1, 0)
+        load_weights(1, 1)
+        load_hidden(0, 2)
+        load_weights(1, 2)
+        load_weights(1, 3)
+        load_hidden(0, 3)
+        we_raw = raw.tile([P, STREAMS * PACK * D], BF16)
+        nc.sync.dma_start(
+            out=we_raw[:].rearrange("p (c n) -> p c n", n=D),
+            in_=We.rearrange("(c p) n -> p c n", p=P),
+        )
+        for q in range(QUARTERS):
+            load_hidden(1, q)
+
+        row_zero = const.tile([P, 2 * D], BF16)
+        nc.vector.memset(row_zero[:], 0.0)
+        bias_rows = const.tile([P, P], BF16)
+        nc.vector.memset(bias_rows[:], 0.0)
+        for s in range(STREAMS):
+            nc.scalar.dma_start(
+                out=bias_rows[D_TILES * s : D_TILES * (s + 1), :], in_=biases[s].rearrange("(m p) -> m p", p=P)
+            )
+        nc.scalar.dma_start(out=row_zero[0:1, 0:D], in_=be.rearrange("(o n) -> o n", o=1))
+        nc.scalar.dma_start(out=row_zero[0:1, D : 2 * D], in_=g_rms.rearrange("(o n) -> o n", o=1))
+
+        eps = const.tile([P, 1], F32)
+        nc.vector.memset(eps[:], EPS)
+        warm = const.tile([P, 1], F32)
+        nc.scalar.activation(out=warm[:], in_=eps[:], func=ACT.Sqrt)
+        ident_f32 = const.tile([P, P], F32)
+        make_identity(nc, ident_f32[:])
+        ident_bf16 = const.tile([P, P], BF16)
+        nc.vector.tensor_copy(out=ident_bf16[:], in_=ident_f32[:])
+        ones = const.tile([P, P], BF16)
+        nc.vector.memset(ones[:], 1.0)
+        b2 = const.tile([P, STREAMS * D_TILES], F32)
+        be_all = const.tile([P, D], F32)
+        g_all = const.tile([P, D], F32)
+
+        def spread_small_vectors():
+            bias_t = work_pool.tile([P, P], BF16, tag="work")
+            nc.tensor.transpose(bias_t[:], bias_rows[:], ident_bf16[:])
+            nc.vector.tensor_copy(out=b2[:], in_=bias_t[:, 0 : STREAMS * D_TILES])
+            for i, dest in enumerate((be_all, g_all)):
+                spread = work_pool.tile([P, D], F32, tag="work")
+                nc.tensor.matmul(
+                    spread[:], lhsT=ones[:], rhs=row_zero[:, D * i : D * (i + 1)], start=True, stop=True
+                )
+                nc.scalar.copy(out=dest[:], in_=spread[:])
+
+        w_codes = [keep.tile([P, PASSES, D], U32, align_bytes=64, name="w_codes_%d" % s) for s in range(STREAMS)]
+        w_scales = [keep.tile([P, PASSES, D], U8, align_bytes=64, name="w_scales_%d" % s) for s in range(STREAMS)]
+        we_codes = keep.tile([P, STREAMS, D], U32, align_bytes=64)
+        we_scales = keep.tile([P, STREAMS, D], U8, align_bytes=64)
+        cat_codes = {}
+        cat_scales = {}
+        h_grouped = {}
+        h_codes = {}
+        h_scales = {}
+        acc = {}
+        waves = {}
+        totals = {}
+
+        def quantise_weights(rows, codes, scales):
+            grouped = stage.tile([P, PACK * D], BF16, align_bytes=64, tag="grouped")
+            regroup(nc.vector.tensor_copy, grouped[:], rows, 0, VECTOR_COLS)
+            regroup(nc.scalar.copy, grouped[:], rows, VECTOR_COLS, D)
+            nc.vector.quantize_mx(out=codes.bitcast(FP8X4), scales=scales, in_=grouped[:])
+
+        def flip_hidden(s, q):
+            words = h_raw[(s, q)][:].bitcast(F32)
+            grouped = stage.tile([P, PASSES * PACK * COLS], BF16, align_bytes=64, tag="h_grouped")
+            pairs = grouped[:].bitcast(F32).rearrange("p (g j r u) -> p g j r u", g=PASSES, j=TILES, u=2)
+            for g in range(PASSES):
+                flipped = work_pool.tile([P, TILES * 2, P], F32, tag="work")
+                for j in range(TILES):
+                    for u in range(2):
+                        first = j * (F // 2) + g * (K_PASS // 2) + u * P
+                        nc.tensor.transpose(flipped[:, 2 * j + u, :], words[:, first : first + P], ident_f32[:])
+                nc.scalar.copy(out=pairs[:, g], in_=flipped[:].rearrange("p (j u) r -> p j r u", u=2))
+            h_grouped[(s, q)] = grouped
+
+        def quantise_hidden(s, q):
+            codes = stage.tile([P, PASSES * COLS], U32, align_bytes=64, tag="h_codes")
+            scales = stage.tile([P, PASSES * COLS], U8, align_bytes=64, tag="h_scales")
+            half = PASSES * COLS // 2
+            for i in range(2):
+                nc.vector.quantize_mx(
+                    out=codes[:, half * i : half * (i + 1)].bitcast(FP8X4),
+                    scales=scales[:, half * i : half * (i + 1)],
+                    in_=h_grouped[(s, q)][:, PACK * half * i : PACK * half * (i + 1)],
+                )
+            h_codes[(s, q)] = codes
+            h_scales[(s, q)] = scales
+
+        def first_stage(s, q):
+            for m in range(D_TILES):
+                acc[m] = acc_pool.tile([P, COLS], F32, name="acc_%d" % m)
+            for g in range(PASSES):
+                for m in range(D_TILES):
+                    rows = slice(P * m, P * (m + 1))
+                    cols = slice(COLS * g, COLS * (g + 1))
+                    nc.tensor.matmul_mx(
+                        out=acc[m][:],
+                        lhsT=w_codes[s][:, g, rows].bitcast(FP8X4),
+                        lhsT_scale=w_scales[s][:, g, rows],
+                        rhs=h_codes[(s, q)][:, cols].bitcast(FP8X4),
+                        rhs_scale=h_scales[(s, q)][:, cols],
+                        start=(g == 0),
+                        stop=(g == PASSES - 1),
+                    )
+
+        def quantise_cat(s, q):
+            plain = stage.tile([P, D_TILES * COLS], BF16, tag="cat_plain")
+            for m in range(D_TILES):
+                nc.scalar.activation(
+                    out=plain[:, COLS * m : COLS * (m + 1)],
+                    in_=acc[m][:],
+                    func=ACT.Identity,
+                    bias=b2[:, D_TILES * s + m : D_TILES * s + m + 1],
+                    scale=1.0,
+                )
+            grouped = stage.tile([P, PACK * COLS], BF16, align_bytes=64, tag="cat_grouped")
+            regroup(nc.vector.tensor_copy, grouped[:], plain[:], 0, COLS)
+            codes = keep.tile([P, COLS], U32, align_bytes=64, name="cat_codes_%d_%d" % (s, q))
+            scales = keep.tile([P, COLS], U8, align_bytes=64, name="cat_scales_%d_%d" % (s, q))
+            nc.vector.quantize_mx(out=codes[:].bitcast(FP8X4), scales=scales[:], in_=grouped[:])
+            cat_codes[(s, q)] = codes
+            cat_scales[(s, q)] = scales
+
+        def second_stage(q):
+            total = tail.tile([P, TILES], F32, tag="total")
+            totals[q] = total
+            for j in range(TILES):
+                cols = slice(P * j, P * (j + 1))
+                y = work_pool.tile([P, D], F32, tag="work")
+                for s in range(STREAMS):
+                    nc.tensor.matmul_mx(
+                        out=y[:],
+                        lhsT=cat_codes[(s, q)][:, cols].bitcast(FP8X4),
+                        lhsT_scale=cat_scales[(s, q)][:, cols],
+                        rhs=we_codes[:, s, :].bitcast(FP8X4),
+                        rhs_scale=we_scales[:, s, :],
+                        start=(s == 0),
+                        stop=(s == STREAMS - 1),
+                    )
+                wave = tail.tile([P, D], F32, tag="wave", bufs=4)
+                nc.vector.tensor_tensor(out=wave[:], in0=y[:], in1=be_all[:], op=ALU.add)
+                squares = tail.tile([P, D], BF16, tag="squares")
+                nc.scalar.activation(
+                    out=squares[:], in_=wave[:], func=ACT.Square, accum_out=totals[q][:, j : j + 1]
+                )
+                waves[(q, j)] = wave
+
+        out_view = out.flatten_outer_dims().rearrange("(p j) d -> p j d", j=TOKEN_TILES)
+
+        def normalise(q):
+            rms = tail.tile([P, TILES], F32, tag="rms")
+            nc.scalar.activation(out=rms[:], in_=totals[q][:], func=ACT.Sqrt, bias=eps[:], scale=1.0 / D)
+            inv = tail.tile([P, TILES], F32, tag="inv")
+            nc.vector.reciprocal(out=inv[:], in_=rms[:])
+            normed = tail.tile([P, TILES, D], F32, tag="normed")
+            for j in range(TILES):
+                nc.vector.scalar_tensor_tensor(
+                    out=normed[:, j, :],
+                    in0=waves[(q, j)][:],
+                    scalar=inv[:, j : j + 1],
+                    in1=g_all[:],
+                    op0=ALU.mult,
+                    op1=ALU.mult,
+                )
+            nc.sync.dma_start(out=out_view[:, TILES * q : TILES * (q + 1), :], in_=normed[:])
+
+        units = [(s, q) for s in range(STREAMS) for q in range(QUARTERS)]
+        for i in range(len(units) + 1):
+            if i < len(units):
+                s, q = units[i]
+                flip_hidden(s, q)
+                if i == 0:
+                    spread_small_vectors()
+                    for g in range(PASSES):
+                        quantise_weights(w_raw[(0, g)][:], w_codes[0][:, g, :], w_scales[0][:, g, :])
+                quantise_hidden(s, q)
+                if i in (1, 2):
+                    for g in (2 * i - 2, 2 * i - 1):
+                        quantise_weights(w_raw[(1, g)][:], w_codes[1][:, g, :], w_scales[1][:, g, :])
+                if i == 3:
+                    for g in range(STREAMS):
+                        quantise_weights(
+                            we_raw[:, PACK * D * g : PACK * D * (g + 1)], we_codes[:, g, :], we_scales[:, g, :]
+                        )
+            if i >= 1:
+                s, q = units[i - 1]
+                first_stage(s, q)
+                quantise_cat(s, q)
+                if s == STREAMS - 1:
+                    second_stage(q)
+                    normalise(q)

@@ -42,15 +42,26 @@ def tile_wavenetworklm_pb_kernel(tc, h_r, h_i, w2r, b2r, w2i, b2i, We, be, g_rms
     hidden = (h_r, h_i)
     weights = (w2r, w2i)
     biases = (b2r, b2i)
+    units = [(s, q) for s in range(STREAMS) for q in range(QUARTERS)]
 
     with ExitStack() as ctx:
+        ctx.enter_context(tc.manual_schedule())
         const = ctx.enter_context(tc.tile_pool(name="const", bufs=1))
         raw = ctx.enter_context(tc.tile_pool(name="raw", bufs=1))
         keep = ctx.enter_context(tc.tile_pool(name="keep", bufs=1))
-        stage = ctx.enter_context(tc.tile_pool(name="stage", bufs=3))
-        tail = ctx.enter_context(tc.tile_pool(name="tail", bufs=2))
+        stage = ctx.enter_context(tc.tile_pool(name="stage", bufs=2))
+        tail = ctx.enter_context(tc.tile_pool(name="tail", bufs=3))
         acc_pool = ctx.enter_context(tc.psum_pool(name="acc", bufs=1))
         work_pool = ctx.enter_context(tc.psum_pool(name="work", bufs=4))
+
+        def chunks_of_step(step):
+            if step == -1:
+                return [(0, g) for g in range(PASSES)]
+            if step in (0, 1):
+                return [(1, 2 * step), (1, 2 * step + 1)]
+            if step in (3, 4):
+                return [(2, step - 3)]
+            return []
 
         h_raw = {}
         w_raw = {}
@@ -61,31 +72,24 @@ def tile_wavenetworklm_pb_kernel(tc, h_r, h_i, w2r, b2r, w2i, b2i, We, be, g_rms
             nc.sync.dma_start(out=t[:], in_=view[:, TILES * F * q : TILES * F * (q + 1)])
             h_raw[(s, q)] = t
 
-        def load_weights(s, g):
-            view = weights[s].rearrange("(c q e) n -> q c (e n)", q=P, e=2)
-            t = raw.tile([P, PACK * D], BF16, name="w_raw_%d_%d" % (s, g))
-            nc.sync.dma_start(
-                out=t[:].rearrange("p (u x) -> p u x", u=2), in_=view[:, 2 * g : 2 * g + 2, :]
-            )
-            w_raw[(s, g)] = t
+        def load_chunk(matrix, g):
+            t = raw.tile([P, PACK * D], BF16, name="w_raw_%d_%d" % (matrix, g))
+            if matrix < STREAMS:
+                view = weights[matrix].rearrange("(c q e) n -> q c (e n)", q=P, e=2)
+                nc.sync.dma_start(
+                    out=t[:].rearrange("p (u x) -> p u x", u=2), in_=view[:, 2 * g : 2 * g + 2, :]
+                )
+            else:
+                view = We.rearrange("(c p) n -> p c n", p=P)
+                nc.sync.dma_start(
+                    out=t[:].rearrange("p (c n) -> p c n", n=D), in_=view[:, PACK * g : PACK * (g + 1), :]
+                )
+            w_raw[(matrix, g)] = t
 
-        load_hidden(0, 0)
-        for g in range(PASSES):
-            load_weights(0, g)
-        load_hidden(0, 1)
-        load_weights(1, 0)
-        load_weights(1, 1)
-        load_hidden(0, 2)
-        load_weights(1, 2)
-        load_weights(1, 3)
-        load_hidden(0, 3)
-        we_raw = raw.tile([P, STREAMS * PACK * D], BF16)
-        nc.sync.dma_start(
-            out=we_raw[:].rearrange("p (c n) -> p c n", n=D),
-            in_=We.rearrange("(c p) n -> p c n", p=P),
-        )
-        for q in range(QUARTERS):
-            load_hidden(1, q)
+        for step in range(-1, len(units) - 1):
+            load_hidden(*units[step + 1])
+            for matrix, g in chunks_of_step(step):
+                load_chunk(matrix, g)
 
         row_zero = const.tile([P, 2 * D], BF16)
         nc.vector.memset(row_zero[:], 0.0)
@@ -123,24 +127,33 @@ def tile_wavenetworklm_pb_kernel(tc, h_r, h_i, w2r, b2r, w2i, b2i, We, be, g_rms
                 )
                 nc.scalar.copy(out=dest[:], in_=spread[:])
 
-        w_codes = [keep.tile([P, PASSES, D], U32, align_bytes=64, name="w_codes_%d" % s) for s in range(STREAMS)]
-        w_scales = [keep.tile([P, PASSES, D], U8, align_bytes=64, name="w_scales_%d" % s) for s in range(STREAMS)]
-        we_codes = keep.tile([P, STREAMS, D], U32, align_bytes=64)
-        we_scales = keep.tile([P, STREAMS, D], U8, align_bytes=64)
+        chunks_in = (PASSES, PASSES, STREAMS)
+        w_codes = [keep.tile([P, n, D], U32, align_bytes=64, name="w_codes_%d" % i) for i, n in enumerate(chunks_in)]
+        w_scales = [keep.tile([P, n, D], U8, align_bytes=64, name="w_scales_%d" % i) for i, n in enumerate(chunks_in)]
+        w_grouped = {}
+        cat_plain = {}
         cat_codes = {}
         cat_scales = {}
         h_grouped = {}
         h_codes = {}
         h_scales = {}
         acc = {}
+        y_banks = {}
         waves = {}
         totals = {}
 
-        def quantise_weights(rows, codes, scales):
-            grouped = stage.tile([P, PACK * D], BF16, align_bytes=64, tag="grouped")
-            regroup(nc.vector.tensor_copy, grouped[:], rows, 0, VECTOR_COLS)
-            regroup(nc.scalar.copy, grouped[:], rows, VECTOR_COLS, D)
-            nc.vector.quantize_mx(out=codes.bitcast(FP8X4), scales=scales, in_=grouped[:])
+        def regroup_chunk(matrix, g):
+            grouped = stage.tile([P, PACK * D], BF16, align_bytes=64, tag="w_grouped", bufs=4)
+            regroup(nc.vector.tensor_copy, grouped[:], w_raw[(matrix, g)][:], 0, VECTOR_COLS)
+            regroup(nc.scalar.copy, grouped[:], w_raw[(matrix, g)][:], VECTOR_COLS, D)
+            w_grouped[(matrix, g)] = grouped
+
+        def quantise_chunk(matrix, g):
+            nc.vector.quantize_mx(
+                out=w_codes[matrix][:, g, :].bitcast(FP8X4),
+                scales=w_scales[matrix][:, g, :],
+                in_=w_grouped[(matrix, g)][:],
+            )
 
         def flip_hidden(s, q):
             words = h_raw[(s, q)][:].bitcast(F32)
@@ -168,24 +181,27 @@ def tile_wavenetworklm_pb_kernel(tc, h_r, h_i, w2r, b2r, w2i, b2i, We, be, g_rms
             h_codes[(s, q)] = codes
             h_scales[(s, q)] = scales
 
-        def first_stage(s, q):
+        def first_stage(s, q, by_pass):
             for m in range(D_TILES):
                 acc[m] = acc_pool.tile([P, COLS], F32, name="acc_%d" % m)
-            for g in range(PASSES):
-                for m in range(D_TILES):
-                    rows = slice(P * m, P * (m + 1))
-                    cols = slice(COLS * g, COLS * (g + 1))
-                    nc.tensor.matmul_mx(
-                        out=acc[m][:],
-                        lhsT=w_codes[s][:, g, rows].bitcast(FP8X4),
-                        lhsT_scale=w_scales[s][:, g, rows],
-                        rhs=h_codes[(s, q)][:, cols].bitcast(FP8X4),
-                        rhs_scale=h_scales[(s, q)][:, cols],
-                        start=(g == 0),
-                        stop=(g == PASSES - 1),
-                    )
+            if by_pass:
+                order = [(g, m) for g in range(PASSES) for m in range(D_TILES)]
+            else:
+                order = [(g, m) for m in range(D_TILES) for g in range(PASSES)]
+            for g, m in order:
+                rows = slice(P * m, P * (m + 1))
+                cols = slice(COLS * g, COLS * (g + 1))
+                nc.tensor.matmul_mx(
+                    out=acc[m][:],
+                    lhsT=w_codes[s][:, g, rows].bitcast(FP8X4),
+                    lhsT_scale=w_scales[s][:, g, rows],
+                    rhs=h_codes[(s, q)][:, cols].bitcast(FP8X4),
+                    rhs_scale=h_scales[(s, q)][:, cols],
+                    start=(g == 0),
+                    stop=(g == PASSES - 1),
+                )
 
-        def quantise_cat(s, q):
+        def add_first_bias(s, q):
             plain = stage.tile([P, D_TILES * COLS], BF16, tag="cat_plain")
             for m in range(D_TILES):
                 nc.scalar.activation(
@@ -195,8 +211,11 @@ def tile_wavenetworklm_pb_kernel(tc, h_r, h_i, w2r, b2r, w2i, b2i, We, be, g_rms
                     bias=b2[:, D_TILES * s + m : D_TILES * s + m + 1],
                     scale=1.0,
                 )
+            cat_plain[(s, q)] = plain
+
+        def quantise_cat(s, q):
             grouped = stage.tile([P, PACK * COLS], BF16, align_bytes=64, tag="cat_grouped")
-            regroup(nc.vector.tensor_copy, grouped[:], plain[:], 0, COLS)
+            regroup(nc.vector.tensor_copy, grouped[:], cat_plain[(s, q)][:], 0, COLS)
             codes = keep.tile([P, COLS], U32, align_bytes=64, name="cat_codes_%d_%d" % (s, q))
             scales = keep.tile([P, COLS], U8, align_bytes=64, name="cat_scales_%d_%d" % (s, q))
             nc.vector.quantize_mx(out=codes[:].bitcast(FP8X4), scales=scales[:], in_=grouped[:])
@@ -204,8 +223,6 @@ def tile_wavenetworklm_pb_kernel(tc, h_r, h_i, w2r, b2r, w2i, b2i, We, be, g_rms
             cat_scales[(s, q)] = scales
 
         def second_stage(q):
-            total = tail.tile([P, TILES], F32, tag="total")
-            totals[q] = total
             for j in range(TILES):
                 cols = slice(P * j, P * (j + 1))
                 y = work_pool.tile([P, D], F32, tag="work")
@@ -214,26 +231,35 @@ def tile_wavenetworklm_pb_kernel(tc, h_r, h_i, w2r, b2r, w2i, b2i, We, be, g_rms
                         out=y[:],
                         lhsT=cat_codes[(s, q)][:, cols].bitcast(FP8X4),
                         lhsT_scale=cat_scales[(s, q)][:, cols],
-                        rhs=we_codes[:, s, :].bitcast(FP8X4),
-                        rhs_scale=we_scales[:, s, :],
+                        rhs=w_codes[2][:, s, :].bitcast(FP8X4),
+                        rhs_scale=w_scales[2][:, s, :],
                         start=(s == 0),
                         stop=(s == STREAMS - 1),
                     )
-                wave = tail.tile([P, D], F32, tag="wave", bufs=4)
-                nc.vector.tensor_tensor(out=wave[:], in0=y[:], in1=be_all[:], op=ALU.add)
+                y_banks[(q, j)] = y
+
+        def add_second_bias(q):
+            for j in range(TILES):
+                wave = tail.tile([P, D], F32, tag="wave", bufs=6)
+                nc.vector.tensor_tensor(out=wave[:], in0=y_banks[(q, j)][:], in1=be_all[:], op=ALU.add)
+                waves[(q, j)] = wave
+
+        def root_mean_square(q):
+            total = tail.tile([P, TILES], F32, tag="total")
+            for j in range(TILES):
                 squares = tail.tile([P, D], BF16, tag="squares")
                 nc.scalar.activation(
-                    out=squares[:], in_=wave[:], func=ACT.Square, accum_out=totals[q][:, j : j + 1]
+                    out=squares[:], in_=waves[(q, j)][:], func=ACT.Square, accum_out=total[:, j : j + 1]
                 )
-                waves[(q, j)] = wave
+            rms = tail.tile([P, TILES], F32, tag="rms")
+            nc.scalar.activation(out=rms[:], in_=total[:], func=ACT.Sqrt, bias=eps[:], scale=1.0 / D)
+            totals[q] = rms
 
         out_view = out.flatten_outer_dims().rearrange("(p j) d -> p j d", j=TOKEN_TILES)
 
         def normalise(q):
-            rms = tail.tile([P, TILES], F32, tag="rms")
-            nc.scalar.activation(out=rms[:], in_=totals[q][:], func=ACT.Sqrt, bias=eps[:], scale=1.0 / D)
             inv = tail.tile([P, TILES], F32, tag="inv")
-            nc.vector.reciprocal(out=inv[:], in_=rms[:])
+            nc.vector.reciprocal(out=inv[:], in_=totals[q][:])
             normed = tail.tile([P, TILES, D], F32, tag="normed")
             for j in range(TILES):
                 nc.vector.scalar_tensor_tensor(
@@ -246,28 +272,36 @@ def tile_wavenetworklm_pb_kernel(tc, h_r, h_i, w2r, b2r, w2i, b2i, We, be, g_rms
                 )
             nc.sync.dma_start(out=out_view[:, TILES * q : TILES * (q + 1), :], in_=normed[:])
 
-        units = [(s, q) for s in range(STREAMS) for q in range(QUARTERS)]
-        for i in range(len(units) + 1):
-            if i < len(units):
-                s, q = units[i]
+        def unit_at(i):
+            return [units[i]] if 0 <= i < len(units) else []
+
+        def quarter_at(i):
+            return [q for s, q in unit_at(i) if s == STREAMS - 1]
+
+        for step in range(-1, len(units) + 3):
+            chunks = chunks_of_step(step)
+            for q in quarter_at(step - 2):
+                add_second_bias(q)
+            for s, q in unit_at(step + 1):
                 flip_hidden(s, q)
-                if i == 0:
-                    spread_small_vectors()
-                    for g in range(PASSES):
-                        quantise_weights(w_raw[(0, g)][:], w_codes[0][:, g, :], w_scales[0][:, g, :])
-                quantise_hidden(s, q)
-                if i in (1, 2):
-                    for g in (2 * i - 2, 2 * i - 1):
-                        quantise_weights(w_raw[(1, g)][:], w_codes[1][:, g, :], w_scales[1][:, g, :])
-                if i == 3:
-                    for g in range(STREAMS):
-                        quantise_weights(
-                            we_raw[:, PACK * D * g : PACK * D * (g + 1)], we_codes[:, g, :], we_scales[:, g, :]
-                        )
-            if i >= 1:
-                s, q = units[i - 1]
-                first_stage(s, q)
+            for s, q in unit_at(step - 1):
                 quantise_cat(s, q)
-                if s == STREAMS - 1:
-                    second_stage(q)
-                    normalise(q)
+            for i, chunk in enumerate(chunks):
+                regroup_chunk(*chunk)
+                if i > 0:
+                    quantise_chunk(*chunks[i - 1])
+            if step == -1:
+                spread_small_vectors()
+            for s, q in unit_at(step):
+                first_stage(s, q, by_pass=(step == 0))
+                add_first_bias(s, q)
+            for q in quarter_at(step - 1):
+                second_stage(q)
+            for q in quarter_at(step - 2):
+                root_mean_square(q)
+            for q in quarter_at(step - 3):
+                normalise(q)
+            for chunk in chunks[-1:]:
+                quantise_chunk(*chunk)
+            for s, q in unit_at(step + 1):
+                quantise_hidden(s, q)

@@ -54,14 +54,14 @@ def tile_wavenetworklm_pb_kernel(tc, h_r, h_i, w2r, b2r, w2i, b2i, We, be, g_rms
         acc_pool = ctx.enter_context(tc.psum_pool(name="acc", bufs=1))
         work_pool = ctx.enter_context(tc.psum_pool(name="work", bufs=4))
 
+        later_chunks = [(1, g) for g in range(PASSES)] + [(2, g) for g in range(STREAMS)]
+
         def chunks_of_step(step):
             if step == -1:
                 return [(0, g) for g in range(PASSES)]
-            if step in (0, 1):
-                return [(1, 2 * step), (1, 2 * step + 1)]
-            if step in (3, 4):
-                return [(2, step - 3)]
-            return []
+            if step == 0:
+                return later_chunks[0:2]
+            return later_chunks[step + 1 : step + 2] if step > 0 else []
 
         h_raw = {}
         w_raw = {}
@@ -132,6 +132,7 @@ def tile_wavenetworklm_pb_kernel(tc, h_r, h_i, w2r, b2r, w2i, b2i, We, be, g_rms
         w_scales = [keep.tile([P, n, D], U8, align_bytes=64, name="w_scales_%d" % i) for i, n in enumerate(chunks_in)]
         w_grouped = {}
         cat_plain = {}
+        cat_grouped = {}
         cat_codes = {}
         cat_scales = {}
         h_grouped = {}
@@ -141,6 +142,9 @@ def tile_wavenetworklm_pb_kernel(tc, h_r, h_i, w2r, b2r, w2i, b2i, We, be, g_rms
         y_banks = {}
         waves = {}
         totals = {}
+        roots = {}
+        inverses = {}
+        results = {}
 
         def regroup_chunk(matrix, g):
             grouped = stage.tile([P, PACK * D], BF16, align_bytes=64, tag="w_grouped", bufs=4)
@@ -181,25 +185,21 @@ def tile_wavenetworklm_pb_kernel(tc, h_r, h_i, w2r, b2r, w2i, b2i, We, be, g_rms
             h_codes[(s, q)] = codes
             h_scales[(s, q)] = scales
 
-        def first_stage(s, q, by_pass):
+        def first_stage(s, q):
             for m in range(D_TILES):
                 acc[m] = acc_pool.tile([P, COLS], F32, name="acc_%d" % m)
-            if by_pass:
-                order = [(g, m) for g in range(PASSES) for m in range(D_TILES)]
-            else:
-                order = [(g, m) for m in range(D_TILES) for g in range(PASSES)]
-            for g, m in order:
                 rows = slice(P * m, P * (m + 1))
-                cols = slice(COLS * g, COLS * (g + 1))
-                nc.tensor.matmul_mx(
-                    out=acc[m][:],
-                    lhsT=w_codes[s][:, g, rows].bitcast(FP8X4),
-                    lhsT_scale=w_scales[s][:, g, rows],
-                    rhs=h_codes[(s, q)][:, cols].bitcast(FP8X4),
-                    rhs_scale=h_scales[(s, q)][:, cols],
-                    start=(g == 0),
-                    stop=(g == PASSES - 1),
-                )
+                for g in range(PASSES):
+                    cols = slice(COLS * g, COLS * (g + 1))
+                    nc.tensor.matmul_mx(
+                        out=acc[m][:],
+                        lhsT=w_codes[s][:, g, rows].bitcast(FP8X4),
+                        lhsT_scale=w_scales[s][:, g, rows],
+                        rhs=h_codes[(s, q)][:, cols].bitcast(FP8X4),
+                        rhs_scale=h_scales[(s, q)][:, cols],
+                        start=(g == 0),
+                        stop=(g == PASSES - 1),
+                    )
 
         def add_first_bias(s, q):
             plain = stage.tile([P, D_TILES * COLS], BF16, tag="cat_plain")
@@ -213,9 +213,13 @@ def tile_wavenetworklm_pb_kernel(tc, h_r, h_i, w2r, b2r, w2i, b2i, We, be, g_rms
                 )
             cat_plain[(s, q)] = plain
 
-        def quantise_cat(s, q):
+        def regroup_cat(s, q):
             grouped = stage.tile([P, PACK * COLS], BF16, align_bytes=64, tag="cat_grouped")
             regroup(nc.vector.tensor_copy, grouped[:], cat_plain[(s, q)][:], 0, COLS)
+            cat_grouped[(s, q)] = grouped
+
+        def quantise_cat(s, q):
+            grouped = cat_grouped[(s, q)]
             codes = keep.tile([P, COLS], U32, align_bytes=64, name="cat_codes_%d_%d" % (s, q))
             scales = keep.tile([P, COLS], U8, align_bytes=64, name="cat_scales_%d_%d" % (s, q))
             nc.vector.quantize_mx(out=codes[:].bitcast(FP8X4), scales=scales[:], in_=grouped[:])
@@ -244,33 +248,41 @@ def tile_wavenetworklm_pb_kernel(tc, h_r, h_i, w2r, b2r, w2i, b2i, We, be, g_rms
                 nc.vector.tensor_tensor(out=wave[:], in0=y_banks[(q, j)][:], in1=be_all[:], op=ALU.add)
                 waves[(q, j)] = wave
 
-        def root_mean_square(q):
+        def sum_squares(q):
             total = tail.tile([P, TILES], F32, tag="total")
             for j in range(TILES):
                 squares = tail.tile([P, D], BF16, tag="squares")
                 nc.scalar.activation(
                     out=squares[:], in_=waves[(q, j)][:], func=ACT.Square, accum_out=total[:, j : j + 1]
                 )
+            totals[q] = total
+
+        def root_mean_square(q):
             rms = tail.tile([P, TILES], F32, tag="rms")
-            nc.scalar.activation(out=rms[:], in_=total[:], func=ACT.Sqrt, bias=eps[:], scale=1.0 / D)
-            totals[q] = rms
+            nc.scalar.activation(out=rms[:], in_=totals[q][:], func=ACT.Sqrt, bias=eps[:], scale=1.0 / D)
+            roots[q] = rms
 
         out_view = out.flatten_outer_dims().rearrange("(p j) d -> p j d", j=TOKEN_TILES)
 
-        def normalise(q):
+        def invert_rms(q):
             inv = tail.tile([P, TILES], F32, tag="inv")
-            nc.vector.reciprocal(out=inv[:], in_=totals[q][:])
+            nc.vector.reciprocal(out=inv[:], in_=roots[q][:])
+            inverses[q] = inv
             normed = tail.tile([P, TILES, D], F32, tag="normed")
-            for j in range(TILES):
-                nc.vector.scalar_tensor_tensor(
-                    out=normed[:, j, :],
-                    in0=waves[(q, j)][:],
-                    scalar=inv[:, j : j + 1],
-                    in1=g_all[:],
-                    op0=ALU.mult,
-                    op1=ALU.mult,
-                )
-            nc.sync.dma_start(out=out_view[:, TILES * q : TILES * (q + 1), :], in_=normed[:])
+            results[q] = normed
+
+        def normalise_tile(q, j):
+            nc.vector.scalar_tensor_tensor(
+                out=results[q][:, j, :],
+                in0=waves[(q, j)][:],
+                scalar=inverses[q][:, j : j + 1],
+                in1=g_all[:],
+                op0=ALU.mult,
+                op1=ALU.mult,
+            )
+
+        def store_quarter(q):
+            nc.sync.dma_start(out=out_view[:, TILES * q : TILES * (q + 1), :], in_=results[q][:])
 
         def unit_at(i):
             return [units[i]] if 0 <= i < len(units) else []
@@ -284,24 +296,33 @@ def tile_wavenetworklm_pb_kernel(tc, h_r, h_i, w2r, b2r, w2i, b2i, We, be, g_rms
                 add_second_bias(q)
             for s, q in unit_at(step + 1):
                 flip_hidden(s, q)
+            for q in quarter_at(step - 3):
+                invert_rms(q)
             for s, q in unit_at(step - 1):
-                quantise_cat(s, q)
+                regroup_cat(s, q)
             for i, chunk in enumerate(chunks):
                 regroup_chunk(*chunk)
                 if i > 0:
                     quantise_chunk(*chunks[i - 1])
+            for q in quarter_at(step - 3):
+                normalise_tile(q, 0)
+            for s, q in unit_at(step - 1):
+                quantise_cat(s, q)
+            for q in quarter_at(step - 3):
+                normalise_tile(q, 1)
+                store_quarter(q)
+            for chunk in chunks[-1:]:
+                quantise_chunk(*chunk)
             if step == -1:
                 spread_small_vectors()
+            for q in quarter_at(step - 2):
+                sum_squares(q)
             for s, q in unit_at(step):
-                first_stage(s, q, by_pass=(step == 0))
+                first_stage(s, q)
                 add_first_bias(s, q)
             for q in quarter_at(step - 1):
                 second_stage(q)
             for q in quarter_at(step - 2):
                 root_mean_square(q)
-            for q in quarter_at(step - 3):
-                normalise(q)
-            for chunk in chunks[-1:]:
-                quantise_chunk(*chunk)
             for s, q in unit_at(step + 1):
                 quantise_hidden(s, q)

@@ -26,7 +26,7 @@ TOKEN_TILES = TOKENS // P
 TILES = 2
 QUARTERS = TOKEN_TILES // TILES
 COLS = TILES * P
-VECTOR_COLS = 384
+VECTOR_COLS = 448
 
 FLOPS = 2 * TOKENS * F * D * STREAMS + 2 * TOKENS * (STREAMS * D) * D
 
@@ -144,7 +144,6 @@ def tile_wavenetworklm_pb_kernel(tc, h_r, h_i, w2r, b2r, w2i, b2i, We, be, g_rms
         totals = {}
         roots = {}
         inverses = {}
-        results = {}
 
         def regroup_chunk(matrix, g):
             grouped = stage.tile([P, PACK * D], BF16, align_bytes=64, tag="w_grouped", bufs=4)
@@ -175,13 +174,7 @@ def tile_wavenetworklm_pb_kernel(tc, h_r, h_i, w2r, b2r, w2i, b2i, We, be, g_rms
         def quantise_hidden(s, q):
             codes = stage.tile([P, PASSES * COLS], U32, align_bytes=64, tag="h_codes")
             scales = stage.tile([P, PASSES * COLS], U8, align_bytes=64, tag="h_scales")
-            half = PASSES * COLS // 2
-            for i in range(2):
-                nc.vector.quantize_mx(
-                    out=codes[:, half * i : half * (i + 1)].bitcast(FP8X4),
-                    scales=scales[:, half * i : half * (i + 1)],
-                    in_=h_grouped[(s, q)][:, PACK * half * i : PACK * half * (i + 1)],
-                )
+            nc.vector.quantize_mx(out=codes[:].bitcast(FP8X4), scales=scales[:], in_=h_grouped[(s, q)][:])
             h_codes[(s, q)] = codes
             h_scales[(s, q)] = scales
 
@@ -268,21 +261,18 @@ def tile_wavenetworklm_pb_kernel(tc, h_r, h_i, w2r, b2r, w2i, b2i, We, be, g_rms
             inv = tail.tile([P, TILES], F32, tag="inv")
             nc.vector.reciprocal(out=inv[:], in_=roots[q][:])
             inverses[q] = inv
-            normed = tail.tile([P, TILES, D], F32, tag="normed")
-            results[q] = normed
 
         def normalise_tile(q, j):
+            normed = tail.tile([P, D], F32, tag="normed", bufs=4)
             nc.vector.scalar_tensor_tensor(
-                out=results[q][:, j, :],
+                out=normed[:],
                 in0=waves[(q, j)][:],
                 scalar=inverses[q][:, j : j + 1],
                 in1=g_all[:],
                 op0=ALU.mult,
                 op1=ALU.mult,
             )
-
-        def store_quarter(q):
-            nc.sync.dma_start(out=out_view[:, TILES * q : TILES * (q + 1), :], in_=results[q][:])
+            nc.sync.dma_start(out=out_view[:, TILES * q + j, :], in_=normed[:])
 
         def unit_at(i):
             return [units[i]] if 0 <= i < len(units) else []
@@ -310,7 +300,6 @@ def tile_wavenetworklm_pb_kernel(tc, h_r, h_i, w2r, b2r, w2i, b2i, We, be, g_rms
                 quantise_cat(s, q)
             for q in quarter_at(step - 3):
                 normalise_tile(q, 1)
-                store_quarter(q)
             for chunk in chunks[-1:]:
                 quantise_chunk(*chunk)
             if step == -1:

@@ -26,15 +26,17 @@ TOKEN_TILES = TOKENS // P
 TILES = 2
 QUARTERS = TOKEN_TILES // TILES
 COLS = TILES * P
-VECTOR_COLS = 448
+WORDS = F // 2
+BANKS = 8
+FIRST_STEP = -1
 
 FLOPS = 2 * TOKENS * F * D * STREAMS + 2 * TOKENS * (STREAMS * D) * D
 
 
-def regroup(copy, grouped, rows, first_col, last_col):
+def regroup(nc, grouped, rows):
     src = rows.rearrange("p (t c i) -> p c t i", t=PACK, i=4)
     dst = grouped.rearrange("p (c i t) -> p c t i", i=4, t=PACK)
-    copy(out=dst[:, first_col // 4 : last_col // 4], in_=src[:, first_col // 4 : last_col // 4])
+    nc.vector.tensor_copy(out=dst, in_=src)
 
 
 def tile_wavenetworklm_pb_kernel(tc, h_r, h_i, w2r, b2r, w2i, b2i, We, be, g_rms, out):
@@ -52,44 +54,45 @@ def tile_wavenetworklm_pb_kernel(tc, h_r, h_i, w2r, b2r, w2i, b2i, We, be, g_rms
         stage = ctx.enter_context(tc.tile_pool(name="stage", bufs=2))
         tail = ctx.enter_context(tc.tile_pool(name="tail", bufs=3))
         acc_pool = ctx.enter_context(tc.psum_pool(name="acc", bufs=1))
-        work_pool = ctx.enter_context(tc.psum_pool(name="work", bufs=4))
+        work_pool = ctx.enter_context(tc.psum_pool(name="work", bufs=BANKS - D_TILES))
 
+        first_chunks = [(0, g) for g in range(PASSES)]
         later_chunks = [(1, g) for g in range(PASSES)] + [(2, g) for g in range(STREAMS)]
 
         def chunks_of_step(step):
-            if step == -1:
-                return [(0, g) for g in range(PASSES)]
+            if step == FIRST_STEP:
+                return first_chunks
             if step == 0:
                 return later_chunks[0:2]
-            return later_chunks[step + 1 : step + 2] if step > 0 else []
+            return later_chunks[step + 1 : step + 2]
 
         h_raw = {}
         w_raw = {}
 
         def load_hidden(s, q):
             view = hidden[s].flatten_outer_dims().rearrange("(p j) k -> p (j k)", j=TOKEN_TILES)
-            t = raw.tile([P, TILES * F], BF16, name="h_raw_%d_%d" % (s, q))
-            nc.sync.dma_start(out=t[:], in_=view[:, TILES * F * q : TILES * F * (q + 1)])
-            h_raw[(s, q)] = t
+            rows = raw.tile([P, TILES * F], BF16, name="h_raw_%d_%d" % (s, q))
+            nc.sync.dma_start(out=rows[:], in_=view[:, TILES * F * q : TILES * F * (q + 1)])
+            h_raw[(s, q)] = rows
 
         def load_chunk(matrix, g):
-            t = raw.tile([P, PACK * D], BF16, name="w_raw_%d_%d" % (matrix, g))
+            rows = raw.tile([P, PACK * D], BF16, name="w_raw_%d_%d" % (matrix, g))
             if matrix < STREAMS:
                 view = weights[matrix].rearrange("(c q e) n -> q c (e n)", q=P, e=2)
                 nc.sync.dma_start(
-                    out=t[:].rearrange("p (u x) -> p u x", u=2), in_=view[:, 2 * g : 2 * g + 2, :]
+                    out=rows[:].rearrange("p (u x) -> p u x", u=2), in_=view[:, 2 * g : 2 * g + 2, :]
                 )
             else:
                 view = We.rearrange("(c p) n -> p c n", p=P)
                 nc.sync.dma_start(
-                    out=t[:].rearrange("p (c n) -> p c n", n=D), in_=view[:, PACK * g : PACK * (g + 1), :]
+                    out=rows[:].rearrange("p (c n) -> p c n", n=D), in_=view[:, PACK * g : PACK * (g + 1), :]
                 )
-            w_raw[(matrix, g)] = t
+            w_raw[(matrix, g)] = rows
 
-        for step in range(-1, len(units) - 1):
+        for step in range(FIRST_STEP, len(units) - 1):
             load_hidden(*units[step + 1])
-            for matrix, g in chunks_of_step(step):
-                load_chunk(matrix, g)
+            for chunk in chunks_of_step(step):
+                load_chunk(*chunk)
 
         row_zero = const.tile([P, 2 * D], BF16)
         nc.vector.memset(row_zero[:], 0.0)
@@ -131,14 +134,14 @@ def tile_wavenetworklm_pb_kernel(tc, h_r, h_i, w2r, b2r, w2i, b2i, We, be, g_rms
         w_codes = [keep.tile([P, n, D], U32, align_bytes=64, name="w_codes_%d" % i) for i, n in enumerate(chunks_in)]
         w_scales = [keep.tile([P, n, D], U8, align_bytes=64, name="w_scales_%d" % i) for i, n in enumerate(chunks_in)]
         w_grouped = {}
-        cat_plain = {}
-        cat_grouped = {}
-        cat_codes = {}
-        cat_scales = {}
         h_grouped = {}
         h_codes = {}
         h_scales = {}
         acc = {}
+        cat_plain = {}
+        cat_grouped = {}
+        cat_codes = {}
+        cat_scales = {}
         y_banks = {}
         waves = {}
         totals = {}
@@ -146,9 +149,8 @@ def tile_wavenetworklm_pb_kernel(tc, h_r, h_i, w2r, b2r, w2i, b2i, We, be, g_rms
         inverses = {}
 
         def regroup_chunk(matrix, g):
-            grouped = stage.tile([P, PACK * D], BF16, align_bytes=64, tag="w_grouped", bufs=4)
-            regroup(nc.vector.tensor_copy, grouped[:], w_raw[(matrix, g)][:], 0, VECTOR_COLS)
-            regroup(nc.scalar.copy, grouped[:], w_raw[(matrix, g)][:], VECTOR_COLS, D)
+            grouped = stage.tile([P, PACK * D], BF16, align_bytes=64, tag="w_grouped", bufs=3)
+            regroup(nc, grouped[:], w_raw[(matrix, g)][:])
             w_grouped[(matrix, g)] = grouped
 
         def quantise_chunk(matrix, g):
@@ -166,7 +168,7 @@ def tile_wavenetworklm_pb_kernel(tc, h_r, h_i, w2r, b2r, w2i, b2i, We, be, g_rms
                 flipped = work_pool.tile([P, TILES * 2, P], F32, tag="work")
                 for j in range(TILES):
                     for u in range(2):
-                        first = j * (F // 2) + g * (K_PASS // 2) + u * P
+                        first = j * WORDS + g * (K_PASS // 2) + u * P
                         nc.tensor.transpose(flipped[:, 2 * j + u, :], words[:, first : first + P], ident_f32[:])
                 nc.scalar.copy(out=pairs[:, g], in_=flipped[:].rearrange("p (j u) r -> p j r u", u=2))
             h_grouped[(s, q)] = grouped
@@ -208,14 +210,13 @@ def tile_wavenetworklm_pb_kernel(tc, h_r, h_i, w2r, b2r, w2i, b2i, We, be, g_rms
 
         def regroup_cat(s, q):
             grouped = stage.tile([P, PACK * COLS], BF16, align_bytes=64, tag="cat_grouped")
-            regroup(nc.vector.tensor_copy, grouped[:], cat_plain[(s, q)][:], 0, COLS)
+            regroup(nc, grouped[:], cat_plain[(s, q)][:])
             cat_grouped[(s, q)] = grouped
 
         def quantise_cat(s, q):
-            grouped = cat_grouped[(s, q)]
             codes = keep.tile([P, COLS], U32, align_bytes=64, name="cat_codes_%d_%d" % (s, q))
             scales = keep.tile([P, COLS], U8, align_bytes=64, name="cat_scales_%d_%d" % (s, q))
-            nc.vector.quantize_mx(out=codes[:].bitcast(FP8X4), scales=scales[:], in_=grouped[:])
+            nc.vector.quantize_mx(out=codes[:].bitcast(FP8X4), scales=scales[:], in_=cat_grouped[(s, q)][:])
             cat_codes[(s, q)] = codes
             cat_scales[(s, q)] = scales
 
@@ -237,7 +238,7 @@ def tile_wavenetworklm_pb_kernel(tc, h_r, h_i, w2r, b2r, w2i, b2i, We, be, g_rms
 
         def add_second_bias(q):
             for j in range(TILES):
-                wave = tail.tile([P, D], F32, tag="wave", bufs=6)
+                wave = tail.tile([P, D], F32, tag="wave", bufs=3 * TILES)
                 nc.vector.tensor_tensor(out=wave[:], in0=y_banks[(q, j)][:], in1=be_all[:], op=ALU.add)
                 waves[(q, j)] = wave
 
@@ -255,15 +256,15 @@ def tile_wavenetworklm_pb_kernel(tc, h_r, h_i, w2r, b2r, w2i, b2i, We, be, g_rms
             nc.scalar.activation(out=rms[:], in_=totals[q][:], func=ACT.Sqrt, bias=eps[:], scale=1.0 / D)
             roots[q] = rms
 
-        out_view = out.flatten_outer_dims().rearrange("(p j) d -> p j d", j=TOKEN_TILES)
-
         def invert_rms(q):
             inv = tail.tile([P, TILES], F32, tag="inv")
             nc.vector.reciprocal(out=inv[:], in_=roots[q][:])
             inverses[q] = inv
 
+        out_view = out.flatten_outer_dims().rearrange("(p j) d -> p j d", j=TOKEN_TILES)
+
         def normalise_tile(q, j):
-            normed = tail.tile([P, D], F32, tag="normed", bufs=4)
+            normed = tail.tile([P, D], F32, tag="normed", bufs=2 * TILES)
             nc.vector.scalar_tensor_tensor(
                 out=normed[:],
                 in0=waves[(q, j)][:],
@@ -280,7 +281,7 @@ def tile_wavenetworklm_pb_kernel(tc, h_r, h_i, w2r, b2r, w2i, b2i, We, be, g_rms
         def quarter_at(i):
             return [q for s, q in unit_at(i) if s == STREAMS - 1]
 
-        for step in range(-1, len(units) + 3):
+        for step in range(FIRST_STEP, len(units) + 3):
             chunks = chunks_of_step(step)
             for q in quarter_at(step - 2):
                 add_second_bias(q)
@@ -302,7 +303,7 @@ def tile_wavenetworklm_pb_kernel(tc, h_r, h_i, w2r, b2r, w2i, b2i, We, be, g_rms
                 normalise_tile(q, 1)
             for chunk in chunks[-1:]:
                 quantise_chunk(*chunk)
-            if step == -1:
+            if step == FIRST_STEP:
                 spread_small_vectors()
             for q in quarter_at(step - 2):
                 sum_squares(q)

from contextlib import ExitStack

import concourse.mybir as mybir
from concourse.masks import make_identity

F32 = mybir.dt.float32
BF16 = mybir.dt.bfloat16
U32 = mybir.dt.uint32
U8 = mybir.dt.uint8
FP8X4 = mybir.dt.float8_e4m3fn_x4
ACT = mybir.ActivationFunctionType
ALU = mybir.AluOpType

P = 128
PACK = 4
K_PASS = P * PACK
TOKENS = 1024
F = 2048
D = 512
EPS = 1e-6

STREAMS = 2
PASSES = F // K_PASS
D_TILES = D // P
TOKEN_TILES = TOKENS // P
TILES = 2
QUARTERS = TOKEN_TILES // TILES
COLS = TILES * P
WORDS = F // 2
BANKS = 8
FIRST_STEP = -1

FLOPS = 2 * TOKENS * F * D * STREAMS + 2 * TOKENS * (STREAMS * D) * D


def regroup(nc, grouped, rows):
    src = rows.rearrange("p (t c i) -> p c t i", t=PACK, i=4)
    dst = grouped.rearrange("p (c i t) -> p c t i", i=4, t=PACK)
    nc.vector.tensor_copy(out=dst, in_=src)


def tile_wavenetworklm_pb_kernel(tc, h_r, h_i, w2r, b2r, w2i, b2i, We, be, g_rms, out):
    nc = tc.nc
    hidden = (h_r, h_i)
    weights = (w2r, w2i)
    biases = (b2r, b2i)
    units = [(s, q) for s in range(STREAMS) for q in range(QUARTERS)]

    with ExitStack() as ctx:
        ctx.enter_context(tc.manual_schedule())
        const = ctx.enter_context(tc.tile_pool(name="const", bufs=1))
        raw = ctx.enter_context(tc.tile_pool(name="raw", bufs=1))
        keep = ctx.enter_context(tc.tile_pool(name="keep", bufs=1))
        stage = ctx.enter_context(tc.tile_pool(name="stage", bufs=2))
        tail = ctx.enter_context(tc.tile_pool(name="tail", bufs=3))
        acc_pool = ctx.enter_context(tc.psum_pool(name="acc", bufs=1))
        work_pool = ctx.enter_context(tc.psum_pool(name="work", bufs=BANKS - D_TILES))

        first_chunks = [(0, g) for g in range(PASSES)]
        later_chunks = [(1, g) for g in range(PASSES)] + [(2, g) for g in range(STREAMS)]

        def chunks_of_step(step):
            if step == FIRST_STEP:
                return first_chunks
            if step == 0:
                return later_chunks[0:2]
            return later_chunks[step + 1 : step + 2]

        h_raw = {}
        w_raw = {}

        def load_hidden(s, q):
            view = hidden[s].flatten_outer_dims().rearrange("(p j) k -> p (j k)", j=TOKEN_TILES)
            rows = raw.tile([P, TILES * F], BF16, name="h_raw_%d_%d" % (s, q))
            nc.sync.dma_start(out=rows[:], in_=view[:, TILES * F * q : TILES * F * (q + 1)])
            h_raw[(s, q)] = rows

        def load_chunk(matrix, g):
            rows = raw.tile([P, PACK * D], BF16, name="w_raw_%d_%d" % (matrix, g))
            if matrix < STREAMS:
                view = weights[matrix].rearrange("(c q e) n -> q c (e n)", q=P, e=2)
                nc.sync.dma_start(
                    out=rows[:].rearrange("p (u x) -> p u x", u=2), in_=view[:, 2 * g : 2 * g + 2, :]
                )
            else:
                view = We.rearrange("(c p) n -> p c n", p=P)
                nc.sync.dma_start(
                    out=rows[:].rearrange("p (c n) -> p c n", n=D), in_=view[:, PACK * g : PACK * (g + 1), :]
                )
            w_raw[(matrix, g)] = rows

        for step in range(FIRST_STEP, len(units) - 1):
            load_hidden(*units[step + 1])
            for chunk in chunks_of_step(step):
                load_chunk(*chunk)

        row_zero = const.tile([P, 2 * D], BF16)
        nc.vector.memset(row_zero[:], 0.0)
        bias_rows = const.tile([P, P], BF16)
        nc.vector.memset(bias_rows[:], 0.0)
        for s in range(STREAMS):
            nc.scalar.dma_start(
                out=bias_rows[D_TILES * s : D_TILES * (s + 1), :], in_=biases[s].rearrange("(m p) -> m p", p=P)
            )
        nc.scalar.dma_start(out=row_zero[0:1, 0:D], in_=be.rearrange("(o n) -> o n", o=1))
        nc.scalar.dma_start(out=row_zero[0:1, D : 2 * D], in_=g_rms.rearrange("(o n) -> o n", o=1))

        eps = const.tile([P, 1], F32)
        nc.vector.memset(eps[:], EPS)
        warm = const.tile([P, 1], F32)
        nc.scalar.activation(out=warm[:], in_=eps[:], func=ACT.Sqrt)
        ident_f32 = const.tile([P, P], F32)
        make_identity(nc, ident_f32[:])
        ident_bf16 = const.tile([P, P], BF16)
        nc.vector.tensor_copy(out=ident_bf16[:], in_=ident_f32[:])
        ones = const.tile([P, P], BF16)
        nc.vector.memset(ones[:], 1.0)
        b2 = const.tile([P, STREAMS * D_TILES], F32)
        be_all = const.tile([P, D], F32)
        g_all = const.tile([P, D], F32)

        def spread_small_vectors():
            bias_t = work_pool.tile([P, P], BF16, tag="work")
            nc.tensor.transpose(bias_t[:], bias_rows[:], ident_bf16[:])
            nc.vector.tensor_copy(out=b2[:], in_=bias_t[:, 0 : STREAMS * D_TILES])
            for i, dest in enumerate((be_all, g_all)):
                spread = work_pool.tile([P, D], F32, tag="work")
                nc.tensor.matmul(
                    spread[:], lhsT=ones[:], rhs=row_zero[:, D * i : D * (i + 1)], start=True, stop=True
                )
                nc.scalar.copy(out=dest[:], in_=spread[:])

        chunks_in = (PASSES, PASSES, STREAMS)
        w_codes = [keep.tile([P, n, D], U32, align_bytes=64, name="w_codes_%d" % i) for i, n in enumerate(chunks_in)]
        w_scales = [keep.tile([P, n, D], U8, align_bytes=64, name="w_scales_%d" % i) for i, n in enumerate(chunks_in)]
        w_grouped = {}
        h_grouped = {}
        h_codes = {}
        h_scales = {}
        acc = {}
        cat_plain = {}
        cat_grouped = {}
        cat_codes = {}
        cat_scales = {}
        y_banks = {}
        waves = {}
        totals = {}
        roots = {}
        inverses = {}

        def regroup_chunk(matrix, g):
            grouped = stage.tile([P, PACK * D], BF16, align_bytes=64, tag="w_grouped", bufs=3)
            regroup(nc, grouped[:], w_raw[(matrix, g)][:])
            w_grouped[(matrix, g)] = grouped

        def quantise_chunk(matrix, g):
            nc.vector.quantize_mx(
                out=w_codes[matrix][:, g, :].bitcast(FP8X4),
                scales=w_scales[matrix][:, g, :],
                in_=w_grouped[(matrix, g)][:],
            )

        def flip_hidden(s, q):
            words = h_raw[(s, q)][:].bitcast(F32)
            grouped = stage.tile([P, PASSES * PACK * COLS], BF16, align_bytes=64, tag="h_grouped")
            pairs = grouped[:].bitcast(F32).rearrange("p (g j r u) -> p g j r u", g=PASSES, j=TILES, u=2)
            for g in range(PASSES):
                flipped = work_pool.tile([P, TILES * 2, P], F32, tag="work")
                for j in range(TILES):
                    for u in range(2):
                        first = j * WORDS + g * (K_PASS // 2) + u * P
                        nc.tensor.transpose(flipped[:, 2 * j + u, :], words[:, first : first + P], ident_f32[:])
                nc.scalar.copy(out=pairs[:, g], in_=flipped[:].rearrange("p (j u) r -> p j r u", u=2))
            h_grouped[(s, q)] = grouped

        def quantise_hidden(s, q):
            codes = stage.tile([P, PASSES * COLS], U32, align_bytes=64, tag="h_codes")
            scales = stage.tile([P, PASSES * COLS], U8, align_bytes=64, tag="h_scales")
            nc.vector.quantize_mx(out=codes[:].bitcast(FP8X4), scales=scales[:], in_=h_grouped[(s, q)][:])
            h_codes[(s, q)] = codes
            h_scales[(s, q)] = scales

        def first_stage(s, q):
            for m in range(D_TILES):
                acc[m] = acc_pool.tile([P, COLS], F32, name="acc_%d" % m)
                rows = slice(P * m, P * (m + 1))
                for g in range(PASSES):
                    cols = slice(COLS * g, COLS * (g + 1))
                    nc.tensor.matmul_mx(
                        out=acc[m][:],
                        lhsT=w_codes[s][:, g, rows].bitcast(FP8X4),
                        lhsT_scale=w_scales[s][:, g, rows],
                        rhs=h_codes[(s, q)][:, cols].bitcast(FP8X4),
                        rhs_scale=h_scales[(s, q)][:, cols],
                        start=(g == 0),
                        stop=(g == PASSES - 1),
                    )

        def add_first_bias(s, q):
            plain = stage.tile([P, D_TILES * COLS], BF16, tag="cat_plain")
            for m in range(D_TILES):
                nc.scalar.activation(
                    out=plain[:, COLS * m : COLS * (m + 1)],
                    in_=acc[m][:],
                    func=ACT.Identity,
                    bias=b2[:, D_TILES * s + m : D_TILES * s + m + 1],
                    scale=1.0,
                )
            cat_plain[(s, q)] = plain

        def regroup_cat(s, q):
            grouped = stage.tile([P, PACK * COLS], BF16, align_bytes=64, tag="cat_grouped")
            regroup(nc, grouped[:], cat_plain[(s, q)][:])
            cat_grouped[(s, q)] = grouped

        def quantise_cat(s, q):
            codes = keep.tile([P, COLS], U32, align_bytes=64, name="cat_codes_%d_%d" % (s, q))
            scales = keep.tile([P, COLS], U8, align_bytes=64, name="cat_scales_%d_%d" % (s, q))
            nc.vector.quantize_mx(out=codes[:].bitcast(FP8X4), scales=scales[:], in_=cat_grouped[(s, q)][:])
            cat_codes[(s, q)] = codes
            cat_scales[(s, q)] = scales

        def second_stage(q):
            for j in range(TILES):
                cols = slice(P * j, P * (j + 1))
                y = work_pool.tile([P, D], F32, tag="work")
                for s in range(STREAMS):
                    nc.tensor.matmul_mx(
                        out=y[:],
                        lhsT=cat_codes[(s, q)][:, cols].bitcast(FP8X4),
                        lhsT_scale=cat_scales[(s, q)][:, cols],
                        rhs=w_codes[2][:, s, :].bitcast(FP8X4),
                        rhs_scale=w_scales[2][:, s, :],
                        start=(s == 0),
                        stop=(s == STREAMS - 1),
                    )
                y_banks[(q, j)] = y

        def add_second_bias(q):
            for j in range(TILES):
                wave = tail.tile([P, D], F32, tag="wave", bufs=3 * TILES)
                nc.vector.tensor_tensor(out=wave[:], in0=y_banks[(q, j)][:], in1=be_all[:], op=ALU.add)
                waves[(q, j)] = wave

        def sum_squares(q):
            total = tail.tile([P, TILES], F32, tag="total")
            for j in range(TILES):
                squares = tail.tile([P, D], BF16, tag="squares")
                nc.scalar.activation(
                    out=squares[:], in_=waves[(q, j)][:], func=ACT.Square, accum_out=total[:, j : j + 1]
                )
            totals[q] = total

        def root_mean_square(q):
            rms = tail.tile([P, TILES], F32, tag="rms")
            nc.scalar.activation(out=rms[:], in_=totals[q][:], func=ACT.Sqrt, bias=eps[:], scale=1.0 / D)
            roots[q] = rms

        def invert_rms(q):
            inv = tail.tile([P, TILES], F32, tag="inv")
            nc.vector.reciprocal(out=inv[:], in_=roots[q][:])
            inverses[q] = inv

        out_view = out.flatten_outer_dims().rearrange("(p j) d -> p j d", j=TOKEN_TILES)

        def normalise_tile(q, j):
            normed = tail.tile([P, D], F32, tag="normed", bufs=2 * TILES)
            nc.vector.scalar_tensor_tensor(
                out=normed[:],
                in0=waves[(q, j)][:],
                scalar=inverses[q][:, j : j + 1],
                in1=g_all[:],
                op0=ALU.mult,
                op1=ALU.mult,
            )
            nc.sync.dma_start(out=out_view[:, TILES * q + j, :], in_=normed[:])

        def unit_at(i):
            return [units[i]] if 0 <= i < len(units) else []

        def quarter_at(i):
            return [q for s, q in unit_at(i) if s == STREAMS - 1]

        for step in range(FIRST_STEP, len(units) + 3):
            chunks = chunks_of_step(step)
            for q in quarter_at(step - 2):
                add_second_bias(q)
            for s, q in unit_at(step + 1):
                flip_hidden(s, q)
            for q in quarter_at(step - 3):
                invert_rms(q)
            for s, q in unit_at(step - 1):
                regroup_cat(s, q)
            for i, chunk in enumerate(chunks):
                regroup_chunk(*chunk)
                if i > 0:
                    quantise_chunk(*chunks[i - 1])
            for q in quarter_at(step - 3):
                normalise_tile(q, 0)
            for s, q in unit_at(step - 1):
                quantise_cat(s, q)
            for q in quarter_at(step - 3):
                normalise_tile(q, 1)
            for chunk in chunks[-1:]:
                quantise_chunk(*chunk)
            if step == FIRST_STEP:
                spread_small_vectors()
            for q in quarter_at(step - 2):
                sum_squares(q)
            for s, q in unit_at(step):
                first_stage(s, q)
                add_first_bias(s, q)
            for q in quarter_at(step - 1):
                second_stage(q)
            for q in quarter_at(step - 2):
                root_mean_square(q)
            for s, q in unit_at(step + 1):
                quantise_hidden(s, q)
